import numpy as np
import ml_dtypes


def mxq(x, axis, fmt="e4m3"):
    dtype, down = {"e4m3": (ml_dtypes.float8_e4m3fn, 7), "e5m2": (ml_dtypes.float8_e5m2, 14)}[fmt]
    v = np.moveaxis(np.asarray(x, np.float32).astype(ml_dtypes.bfloat16).astype(np.float64), axis, -1)
    blocks = v.reshape(v.shape[:-1] + (-1, 32))
    amax = np.abs(blocks).max(-1, keepdims=True)
    byte = np.maximum(np.where(amax > 0, np.frexp(amax)[1] - 1 + 127, 0) - down, 1)
    scale = np.exp2(byte - 127.0)
    codes = (blocks / scale).astype(np.float32).astype(dtype).astype(np.float64)
    return np.moveaxis((codes * scale).reshape(v.shape), -1, axis)


WIDE = False


def mx_kscale(k):
    if not WIDE:
        return np.ones(k)
    levels = np.array([10, -10, 5, -5, 0])
    a = np.random.permutation(np.resize(levels, k // 512 * 4)).reshape(k // 512, 4)
    idx = np.arange(k)
    return np.exp2(a[idx // 512, idx % 128 // 32])


BF16 = ml_dtypes.bfloat16


def bf(x):
    return np.asarray(x, np.float32).astype(BF16)


def f64(x):
    return np.asarray(x).astype(np.float64)


B, C, H, W = 16, 512, 16, 32
HW = H * W


def setup_inputs():
    s = mx_kscale(C)
    return {"x": bf(np.random.standard_normal((B, C, H, W)) * s[None, :, None, None]),
            "m": bf(0.5 * HW / B + np.random.standard_normal((B, HW))),
            "w_mask": bf(np.random.standard_normal((C, C)) * 0.5 * HW / np.sqrt(C) / s[None, :])}


def reference(x, m, w_mask):
    mm = f64(m)
    e = np.exp(mm - mm.max(axis=-1, keepdims=True))
    attn = (e / e.sum(axis=-1, keepdims=True)).reshape(B, 1, H, W)
    gated = (f64(x) * attn).reshape(B, C, HW)
    y = mxq(f64(w_mask), 1, "e4m3") @ mxq(gated, 1, "e4m3")
    return y.reshape(B, C, H, W)

@@ -1,0 +1,132 @@
+from contextlib import ExitStack
+
+import concourse.mybir as mybir
+from concourse.masks import make_identity
+
+F32 = mybir.dt.float32
+BF16 = mybir.dt.bfloat16
+U32 = mybir.dt.uint32
+U8 = mybir.dt.uint8
+FP8X4 = mybir.dt.float8_e4m3fn_x4
+
+P = 128
+PACK = 4
+B = 16
+C = 512
+PIX = 512
+D_TILES = C // P
+
+FLOPS = 2 * B * C * C * PIX
+
+
+def tile_nlgp_pb_t_kernel(tc, x, m, w_mask, out):
+    nc = tc.nc
+    with ExitStack() as ctx:
+        ctx.enter_context(tc.manual_schedule())
+        const = ctx.enter_context(tc.tile_pool(name="const", bufs=1))
+        x_pool = ctx.enter_context(tc.tile_pool(name="x_pool", bufs=B))
+        y_pool = ctx.enter_context(tc.tile_pool(name="y_pool", bufs=3))
+        res_pool = ctx.enter_context(tc.tile_pool(name="res_pool", bufs=6))
+        psum_gate = ctx.enter_context(tc.psum_pool(name="psum_gate", bufs=3))
+        psum_acc = ctx.enter_context(tc.psum_pool(name="psum_acc", bufs=5))
+
+        m_sb = const.tile([B, PIX], BF16)
+        nc.sync.dma_start(out=m_sb[:], in_=m)
+        w_sb = const.tile([P, D_TILES * C], BF16)
+        nc.sync.dma_start(out=w_sb[:], in_=w_mask.rearrange("(r i) c -> r (i c)", i=D_TILES))
+        x_sb = []
+        for b in range(B):
+            x_b = x_pool.tile([P, PACK * PIX], BF16, tag="x", name="x_b")
+            nc.sync.dma_start(out=x_b[:], in_=x[b].rearrange("(p j) h w -> p (j h w)", j=PACK))
+            x_sb.append(x_b)
+
+        ident = const.tile([P, P], F32)
+        make_identity(nc, ident[:])
+        zero_col = const.tile([P, 1], F32)
+        nc.vector.memset(zero_col[:], 0.0)
+        one_col = const.tile([P, 1], F32)
+        nc.scalar.activation(out=one_col[:], in_=zero_col[:], func=mybir.ActivationFunctionType.Exp)
+        attn = const.tile([P, PIX], F32)
+        nc.vector.memset(attn[:], 0.0)
+
+        neg_max = const.tile([B, 1], F32)
+        nc.vector.reduce_max(out=neg_max[:], in_=m_sb[:], axis=mybir.AxisListType.X, negate=True)
+        e = const.tile([B, PIX], F32)
+        e_sum = const.tile([B, 1], F32)
+        nc.scalar.activation(
+            out=e[:],
+            in_=m_sb[:],
+            func=mybir.ActivationFunctionType.Exp,
+            bias=neg_max[:],
+            scale=1.0,
+            accum_out=e_sum[:],
+        )
+        inv_sum = const.tile([B, 1], F32)
+        nc.vector.reciprocal(out=inv_sum[:], in_=e_sum[:])
+        nc.vector.tensor_scalar_mul(out=attn[0:B, :], in0=e[:], scalar1=inv_sum[:])
+
+        w_words = w_sb[:].bitcast(F32).rearrange("r (i p u) -> r i u p", i=D_TILES, u=2)
+        w_grouped = const.tile([P, D_TILES * P * PACK], BF16, align_bytes=64)
+        w_grouped_words = w_grouped[:].bitcast(F32).rearrange("p (i r u) -> p i r u", i=D_TILES, u=2)
+        for half in range(2):
+            w_t = psum_gate.tile([P, 2, 2, P], F32, tag="gate", name="w_t")
+            for i2 in range(2):
+                for u in range(2):
+                    nc.tensor.transpose(w_t[:, i2, u, :], w_words[:, 2 * half + i2, u, :], ident[:])
+            nc.scalar.copy(
+                out=w_grouped_words[:, 2 * half : 2 * half + 2, :, :],
+                in_=w_t[:].rearrange("p i u r -> p i r u"),
+            )
+        w_codes = const.tile([P, D_TILES * P], U32, align_bytes=64)
+        w_scales = const.tile([P, D_TILES * P], U8, align_bytes=64)
+        nc.vector.quantize_mx(out=w_codes[:].bitcast(FP8X4), scales=w_scales[:], in_=w_grouped[:])
+
+        def gate(b):
+            attn_all = psum_gate.tile([P, PIX], F32, tag="gate", name="attn_all")
+            nc.tensor.matmul(
+                out=attn_all[:],
+                lhsT=ident[:, b : b + 1].to_broadcast([P, P]),
+                rhs=attn[:],
+                start=True,
+                stop=True,
+            )
+            y = y_pool.tile([P, PIX, PACK], BF16, align_bytes=64, tag="y", name="y")
+            nc.vector.tensor_tensor(
+                out=y[:],
+                in0=x_sb[b][:].rearrange("p (j w) -> p w j", j=PACK),
+                in1=attn_all[:].unsqueeze(2).to_broadcast([P, PIX, PACK]),
+                op=mybir.AluOpType.mult,
+            )
+            return y
+
+        def convolve(b, y):
+            y_codes = y_pool.tile([P, PIX], U32, align_bytes=64, tag="y_codes", name="y_codes")
+            y_scales = y_pool.tile([P, PIX], U8, align_bytes=64, tag="y_scales", name="y_scales")
+            nc.vector.quantize_mx(
+                out=y_codes[:].bitcast(FP8X4),
+                scales=y_scales[:],
+                in_=y[:].rearrange("p w j -> p (w j)"),
+            )
+            res = res_pool.tile([P, D_TILES, PIX], F32, tag="res", name="res")
+            for i in range(D_TILES):
+                acc = psum_acc.tile([P, PIX], F32, tag="acc", name="acc")
+                nc.tensor.matmul_mx(
+                    out=acc[:],
+                    lhsT=w_codes[:, i * P : (i + 1) * P].bitcast(FP8X4),
+                    lhsT_scale=w_scales[:, i * P : (i + 1) * P],
+                    rhs=y_codes[:].bitcast(FP8X4),
+                    rhs_scale=y_scales[:],
+                    start=True,
+                    stop=True,
+                )
+                nc.scalar.copy(out=res[:, i, :], in_=acc[:])
+            nc.sync.dma_start(
+                out=out[b].rearrange("(r i) h w -> r (i h w)", i=D_TILES),
+                in_=res[:].rearrange("r i w -> r (i w)"),
+            )
+
+        y_now = gate(0)
+        for b in range(B):
+            y_next = gate(b + 1) if b + 1 < B else None
+            convolve(b, y_now)
+            y_now = y_next

@@ -81,7 +81,7 @@ def tile_nlgp_pb_t_kernel(tc, x, m, w_mask, out):
         w_scales = const.tile([P, D_TILES * P], U8, align_bytes=64)
         nc.vector.quantize_mx(out=w_codes[:].bitcast(FP8X4), scales=w_scales[:], in_=w_grouped[:])
 
-        def gate(b):
+        def spread(b):
             attn_all = psum_gate.tile([P, PIX], F32, tag="gate", name="attn_all")
             nc.tensor.matmul(
                 out=attn_all[:],
@@ -90,6 +90,9 @@ def tile_nlgp_pb_t_kernel(tc, x, m, w_mask, out):
                 start=True,
                 stop=True,
             )
+            return attn_all
+
+        def gate(b, attn_all):
             y = y_pool.tile([P, PIX, PACK], BF16, align_bytes=64, tag="y", name="y")
             nc.vector.tensor_tensor(
                 out=y[:],
@@ -125,8 +128,11 @@ def tile_nlgp_pb_t_kernel(tc, x, m, w_mask, out):
                 in_=res[:].rearrange("r i w -> r (i w)"),
             )
 
-        y_now = gate(0)
+        attn_of = {0: spread(0), 1: spread(1)}
+        y_of = {0: gate(0, attn_of[0])}
         for b in range(B):
-            y_next = gate(b + 1) if b + 1 < B else None
-            convolve(b, y_now)
-            y_now = y_next
+            if b + 2 < B:
+                attn_of[b + 2] = spread(b + 2)
+            if b + 1 < B:
+                y_of[b + 1] = gate(b + 1, attn_of[b + 1])
+            convolve(b, y_of[b])

@@ -15,6 +15,8 @@ B = 16
 C = 512
 PIX = 512
 D_TILES = C // P
+AHEAD = 3
+ACC_BANKS = 8 - AHEAD
 
 FLOPS = 2 * B * C * C * PIX
 
@@ -27,8 +29,8 @@ def tile_nlgp_pb_t_kernel(tc, x, m, w_mask, out):
         x_pool = ctx.enter_context(tc.tile_pool(name="x_pool", bufs=B))
         y_pool = ctx.enter_context(tc.tile_pool(name="y_pool", bufs=3))
         res_pool = ctx.enter_context(tc.tile_pool(name="res_pool", bufs=6))
-        psum_gate = ctx.enter_context(tc.psum_pool(name="psum_gate", bufs=3))
-        psum_acc = ctx.enter_context(tc.psum_pool(name="psum_acc", bufs=5))
+        psum_gate = ctx.enter_context(tc.psum_pool(name="psum_gate", bufs=AHEAD))
+        psum_acc = ctx.enter_context(tc.psum_pool(name="psum_acc", bufs=ACC_BANKS))
 
         m_sb = const.tile([B, PIX], BF16)
         nc.sync.dma_start(out=m_sb[:], in_=m)
@@ -111,6 +113,9 @@ def tile_nlgp_pb_t_kernel(tc, x, m, w_mask, out):
                 in_=y[:].rearrange("p w j -> p (w j)"),
             )
             res = res_pool.tile([P, D_TILES, PIX], F32, tag="res", name="res")
+            out_b = out[b].rearrange("(r i) h w -> r i (h w)", i=D_TILES)
+            last = b == B - 1
+            tiles_a_store = D_TILES // 2 if last else D_TILES
             for i in range(D_TILES):
                 acc = psum_acc.tile([P, PIX], F32, tag="acc", name="acc")
                 nc.tensor.matmul_mx(
@@ -122,17 +127,23 @@ def tile_nlgp_pb_t_kernel(tc, x, m, w_mask, out):
                     start=True,
                     stop=True,
                 )
-                nc.scalar.copy(out=res[:, i, :], in_=acc[:])
-            nc.sync.dma_start(
-                out=out[b].rearrange("(r i) h w -> r (i h w)", i=D_TILES),
-                in_=res[:].rearrange("r i w -> r (i w)"),
-            )
+                if last and i % 2 == 1:
+                    nc.vector.tensor_copy(out=res[:, i, :], in_=acc[:])
+                else:
+                    nc.scalar.copy(out=res[:, i, :], in_=acc[:])
+                if (i + 1) % tiles_a_store == 0:
+                    stored = slice(i + 1 - tiles_a_store, i + 1)
+                    nc.sync.dma_start(out=out_b[:, stored, :], in_=res[:, stored, :])
 
-        attn_of = {0: spread(0), 1: spread(1)}
+        attn_of = {}
+        for b in range(AHEAD):
+            attn_of[b] = spread(b)
         y_of = {0: gate(0, attn_of[0])}
         for b in range(B):
-            if b + 2 < B:
-                attn_of[b + 2] = spread(b + 2)
-            if b + 1 < B:
+            if b + AHEAD < B:
+                attn_of[b + AHEAD] = spread(b + AHEAD)
+            if b + 1 < B - 1:
                 y_of[b + 1] = gate(b + 1, attn_of[b + 1])
             convolve(b, y_of[b])
+            if b + 1 == B - 1:
+                y_of[b + 1] = gate(b + 1, attn_of[b + 1])

@@ -15,6 +15,7 @@ B = 16
 C = 512
 PIX = 512
 D_TILES = C // P
+RUN = 4
 AHEAD = 3
 ACC_BANKS = 8 - AHEAD
 
@@ -97,9 +98,12 @@ def tile_nlgp_pb_t_kernel(tc, x, m, w_mask, out):
         def gate(b, attn_all):
             y = y_pool.tile([P, PIX, PACK], BF16, align_bytes=64, tag="y", name="y")
             nc.vector.tensor_tensor(
-                out=y[:],
-                in0=x_sb[b][:].rearrange("p (j w) -> p w j", j=PACK),
-                in1=attn_all[:].unsqueeze(2).to_broadcast([P, PIX, PACK]),
+                out=y[:].rearrange("p (g i) j -> p g j i", i=RUN),
+                in0=x_sb[b][:].rearrange("p (j g i) -> p g j i", j=PACK, i=RUN),
+                in1=attn_all[:]
+                .rearrange("p (g i) -> p g i", i=RUN)
+                .unsqueeze(2)
+                .to_broadcast([P, PIX // RUN, PACK, RUN]),
                 op=mybir.AluOpType.mult,
             )
             return y

@@ -16,6 +16,8 @@ C = 512
 PIX = 512
 D_TILES = C // P
 RUN = 4
+G_PIX = 128
+V_PIX = PIX - G_PIX
 AHEAD = 3
 ACC_BANKS = 8 - AHEAD
 
@@ -29,6 +31,7 @@ def tile_nlgp_pb_t_kernel(tc, x, m, w_mask, out):
         const = ctx.enter_context(tc.tile_pool(name="const", bufs=1))
         x_pool = ctx.enter_context(tc.tile_pool(name="x_pool", bufs=B))
         y_pool = ctx.enter_context(tc.tile_pool(name="y_pool", bufs=3))
+        attn_pool = ctx.enter_context(tc.tile_pool(name="attn_pool", bufs=AHEAD + 1))
         res_pool = ctx.enter_context(tc.tile_pool(name="res_pool", bufs=6))
         psum_gate = ctx.enter_context(tc.psum_pool(name="psum_gate", bufs=AHEAD))
         psum_acc = ctx.enter_context(tc.psum_pool(name="psum_acc", bufs=ACC_BANKS))
@@ -93,17 +96,32 @@ def tile_nlgp_pb_t_kernel(tc, x, m, w_mask, out):
                 start=True,
                 stop=True,
             )
-            return attn_all
+            attn_g = attn_pool.tile([P, G_PIX], F32, tag="attn_g", name="attn_g")
+            nc.scalar.copy(out=attn_g[:], in_=attn_all[:, V_PIX:PIX])
+            return attn_all, attn_g
 
-        def gate(b, attn_all):
+        def gate(b, attn_all, attn_g):
             y = y_pool.tile([P, PIX, PACK], BF16, align_bytes=64, tag="y", name="y")
-            nc.vector.tensor_tensor(
-                out=y[:].rearrange("p (g i) j -> p g j i", i=RUN),
-                in0=x_sb[b][:].rearrange("p (j g i) -> p g j i", j=PACK, i=RUN),
-                in1=attn_all[:]
+            y_runs = y[:].rearrange("p (g i) j -> p g j i", i=RUN)
+            x_runs = x_sb[b][:].rearrange("p (j g i) -> p g j i", j=PACK, i=RUN)
+            v_runs = V_PIX // RUN
+            g_runs = G_PIX // RUN
+            nc.gpsimd.tensor_tensor(
+                out=y_runs[:, v_runs:, :, :],
+                in0=x_runs[:, v_runs:, :, :],
+                in1=attn_g[:]
                 .rearrange("p (g i) -> p g i", i=RUN)
                 .unsqueeze(2)
-                .to_broadcast([P, PIX // RUN, PACK, RUN]),
+                .to_broadcast([P, g_runs, PACK, RUN]),
+                op=mybir.AluOpType.mult,
+            )
+            nc.vector.tensor_tensor(
+                out=y_runs[:, :v_runs, :, :],
+                in0=x_runs[:, :v_runs, :, :],
+                in1=attn_all[:, 0:V_PIX]
+                .rearrange("p (g i) -> p g i", i=RUN)
+                .unsqueeze(2)
+                .to_broadcast([P, v_runs, PACK, RUN]),
                 op=mybir.AluOpType.mult,
             )
             return y
@@ -142,12 +160,12 @@ def tile_nlgp_pb_t_kernel(tc, x, m, w_mask, out):
         attn_of = {}
         for b in range(AHEAD):
             attn_of[b] = spread(b)
-        y_of = {0: gate(0, attn_of[0])}
+        y_of = {0: gate(0, *attn_of[0])}
         for b in range(B):
             if b + AHEAD < B:
                 attn_of[b + AHEAD] = spread(b + AHEAD)
             if b + 1 < B - 1:
-                y_of[b + 1] = gate(b + 1, attn_of[b + 1])
+                y_of[b + 1] = gate(b + 1, *attn_of[b + 1])
             convolve(b, y_of[b])
             if b + 1 == B - 1:
-                y_of[b + 1] = gate(b + 1, attn_of[b + 1])
+                y_of[b + 1] = gate(b + 1, *attn_of[b + 1])

@@ -135,9 +135,6 @@ def tile_nlgp_pb_t_kernel(tc, x, m, w_mask, out):
                 in_=y[:].rearrange("p w j -> p (w j)"),
             )
             res = res_pool.tile([P, D_TILES, PIX], F32, tag="res", name="res")
-            out_b = out[b].rearrange("(r i) h w -> r i (h w)", i=D_TILES)
-            last = b == B - 1
-            tiles_a_store = D_TILES // 2 if last else D_TILES
             for i in range(D_TILES):
                 acc = psum_acc.tile([P, PIX], F32, tag="acc", name="acc")
                 nc.tensor.matmul_mx(
@@ -149,13 +146,11 @@ def tile_nlgp_pb_t_kernel(tc, x, m, w_mask, out):
                     start=True,
                     stop=True,
                 )
-                if last and i % 2 == 1:
-                    nc.vector.tensor_copy(out=res[:, i, :], in_=acc[:])
-                else:
-                    nc.scalar.copy(out=res[:, i, :], in_=acc[:])
-                if (i + 1) % tiles_a_store == 0:
-                    stored = slice(i + 1 - tiles_a_store, i + 1)
-                    nc.sync.dma_start(out=out_b[:, stored, :], in_=res[:, stored, :])
+                nc.scalar.copy(out=res[:, i, :], in_=acc[:])
+            nc.sync.dma_start(
+                out=out[b].rearrange("(r i) h w -> r (i h w)", i=D_TILES),
+                in_=res[:].rearrange("r i w -> r (i w)"),
+            )
 
         attn_of = {}
         for b in range(AHEAD):
@@ -164,8 +159,6 @@ def tile_nlgp_pb_t_kernel(tc, x, m, w_mask, out):
         for b in range(B):
             if b + AHEAD < B:
                 attn_of[b + AHEAD] = spread(b + AHEAD)
-            if b + 1 < B - 1:
+            if b + 1 < B:
                 y_of[b + 1] = gate(b + 1, *attn_of[b + 1])
             convolve(b, y_of[b])
-            if b + 1 == B - 1:
-                y_of[b + 1] = gate(b + 1, *attn_of[b + 1])

@@ -38,11 +38,11 @@ def tile_nlgp_pb_t_kernel(tc, x, m, w_mask, out):
 
         m_sb = const.tile([B, PIX], BF16)
         nc.sync.dma_start(out=m_sb[:], in_=m)
-        w_sb = const.tile([P, D_TILES * C], BF16)
+        w_sb = const.tile([P, D_TILES * C], BF16, align_bytes=256)
         nc.sync.dma_start(out=w_sb[:], in_=w_mask.rearrange("(r i) c -> r (i c)", i=D_TILES))
         x_sb = []
         for b in range(B):
-            x_b = x_pool.tile([P, PACK * PIX], BF16, tag="x", name="x_b")
+            x_b = x_pool.tile([P, PACK * PIX], BF16, align_bytes=256, tag="x", name="x_b")
             nc.sync.dma_start(out=x_b[:], in_=x[b].rearrange("(p j) h w -> p (j h w)", j=PACK))
             x_sb.append(x_b)
 
@@ -134,7 +134,7 @@ def tile_nlgp_pb_t_kernel(tc, x, m, w_mask, out):
                 scales=y_scales[:],
                 in_=y[:].rearrange("p w j -> p (w j)"),
             )
-            res = res_pool.tile([P, D_TILES, PIX], F32, tag="res", name="res")
+            res = res_pool.tile([P, D_TILES, PIX], F32, align_bytes=256, tag="res", name="res")
             for i in range(D_TILES):
                 acc = psum_acc.tile([P, PIX], F32, tag="acc", name="acc")
                 nc.tensor.matmul_mx(

@@ -16,7 +16,7 @@ C = 512
 PIX = 512
 D_TILES = C // P
 RUN = 4
-G_PIX = 128
+G_PIX = 96
 V_PIX = PIX - G_PIX
 AHEAD = 3
 ACC_BANKS = 8 - AHEAD

@@ -18,6 +18,7 @@ D_TILES = C // P
 RUN = 4
 G_PIX = 96
 V_PIX = PIX - G_PIX
+LOAD_IMAGES = (1, 1, 2, 4, 4, 4)
 AHEAD = 3
 ACC_BANKS = 8 - AHEAD
 
@@ -29,7 +30,7 @@ def tile_nlgp_pb_t_kernel(tc, x, m, w_mask, out):
     with ExitStack() as ctx:
         ctx.enter_context(tc.manual_schedule())
         const = ctx.enter_context(tc.tile_pool(name="const", bufs=1))
-        x_pool = ctx.enter_context(tc.tile_pool(name="x_pool", bufs=B))
+        x_pool = ctx.enter_context(tc.tile_pool(name="x_pool", bufs=1))
         y_pool = ctx.enter_context(tc.tile_pool(name="y_pool", bufs=3))
         attn_pool = ctx.enter_context(tc.tile_pool(name="attn_pool", bufs=AHEAD + 1))
         res_pool = ctx.enter_context(tc.tile_pool(name="res_pool", bufs=6))
@@ -40,11 +41,14 @@ def tile_nlgp_pb_t_kernel(tc, x, m, w_mask, out):
         nc.sync.dma_start(out=m_sb[:], in_=m)
         w_sb = const.tile([P, D_TILES * C], BF16, align_bytes=256)
         nc.sync.dma_start(out=w_sb[:], in_=w_mask.rearrange("(r i) c -> r (i c)", i=D_TILES))
-        x_sb = []
-        for b in range(B):
-            x_b = x_pool.tile([P, PACK * PIX], BF16, align_bytes=256, tag="x", name="x_b")
-            nc.sync.dma_start(out=x_b[:], in_=x[b].rearrange("(p j) h w -> p (j h w)", j=PACK))
-            x_sb.append(x_b)
+        x_all = x_pool.tile([P, B, PACK * PIX], BF16, align_bytes=256)
+        first = 0
+        for count in LOAD_IMAGES:
+            nc.sync.dma_start(
+                out=x_all[:, first : first + count, :],
+                in_=x[first : first + count].rearrange("b (p j) h w -> p b (j h w)", j=PACK),
+            )
+            first += count
 
         ident = const.tile([P, P], F32)
         make_identity(nc, ident[:])
@@ -103,7 +107,7 @@ def tile_nlgp_pb_t_kernel(tc, x, m, w_mask, out):
         def gate(b, attn_all, attn_g):
             y = y_pool.tile([P, PIX, PACK], BF16, align_bytes=64, tag="y", name="y")
             y_runs = y[:].rearrange("p (g i) j -> p g j i", i=RUN)
-            x_runs = x_sb[b][:].rearrange("p (j g i) -> p g j i", j=PACK, i=RUN)
+            x_runs = x_all[:, b, :].rearrange("p (j g i) -> p g j i", j=PACK, i=RUN)
             v_runs = V_PIX // RUN
             g_runs = G_PIX // RUN
             nc.gpsimd.tensor_tensor(

@@ -33,7 +33,7 @@ def tile_nlgp_pb_t_kernel(tc, x, m, w_mask, out):
         x_pool = ctx.enter_context(tc.tile_pool(name="x_pool", bufs=1))
         y_pool = ctx.enter_context(tc.tile_pool(name="y_pool", bufs=3))
         attn_pool = ctx.enter_context(tc.tile_pool(name="attn_pool", bufs=AHEAD + 1))
-        res_pool = ctx.enter_context(tc.tile_pool(name="res_pool", bufs=6))
+        res_pool = ctx.enter_context(tc.tile_pool(name="res_pool", bufs=12))
         psum_gate = ctx.enter_context(tc.psum_pool(name="psum_gate", bufs=AHEAD))
         psum_acc = ctx.enter_context(tc.psum_pool(name="psum_acc", bufs=ACC_BANKS))
 

@@ -19,6 +19,7 @@ RUN = 4
 G_PIX = 96
 V_PIX = PIX - G_PIX
 LOAD_IMAGES = (1, 1, 2, 4, 4, 4)
+G_GROUP = 4
 AHEAD = 3
 ACC_BANKS = 8 - AHEAD
 
@@ -32,7 +33,6 @@ def tile_nlgp_pb_t_kernel(tc, x, m, w_mask, out):
         const = ctx.enter_context(tc.tile_pool(name="const", bufs=1))
         x_pool = ctx.enter_context(tc.tile_pool(name="x_pool", bufs=1))
         y_pool = ctx.enter_context(tc.tile_pool(name="y_pool", bufs=3))
-        attn_pool = ctx.enter_context(tc.tile_pool(name="attn_pool", bufs=AHEAD + 1))
         res_pool = ctx.enter_context(tc.tile_pool(name="res_pool", bufs=12))
         psum_gate = ctx.enter_context(tc.psum_pool(name="psum_gate", bufs=AHEAD))
         psum_acc = ctx.enter_context(tc.psum_pool(name="psum_acc", bufs=ACC_BANKS))
@@ -92,19 +92,31 @@ def tile_nlgp_pb_t_kernel(tc, x, m, w_mask, out):
         nc.vector.quantize_mx(out=w_codes[:].bitcast(FP8X4), scales=w_scales[:], in_=w_grouped[:])
 
         def spread(b):
-            attn_all = psum_gate.tile([P, PIX], F32, tag="gate", name="attn_all")
+            attn_all = psum_gate.tile([P, V_PIX], F32, tag="gate", name="attn_all")
             nc.tensor.matmul(
                 out=attn_all[:],
                 lhsT=ident[:, b : b + 1].to_broadcast([P, P]),
-                rhs=attn[:],
+                rhs=attn[:, 0:V_PIX],
                 start=True,
                 stop=True,
             )
-            attn_g = attn_pool.tile([P, G_PIX], F32, tag="attn_g", name="attn_g")
-            nc.scalar.copy(out=attn_g[:], in_=attn_all[:, V_PIX:PIX])
-            return attn_all, attn_g
+            return attn_all
 
-        def gate(b, attn_all, attn_g):
+        attn_g_all = const.tile([P, B, G_PIX], F32)
+
+        def spread_for_gpsimd(first):
+            bank = psum_acc.tile([P, G_GROUP, G_PIX], F32, tag="acc", name="bank")
+            for n in range(G_GROUP):
+                nc.tensor.matmul(
+                    out=bank[:, n, :],
+                    lhsT=ident[:, first + n : first + n + 1].to_broadcast([P, P]),
+                    rhs=attn[:, V_PIX:PIX],
+                    start=True,
+                    stop=True,
+                )
+            nc.scalar.copy(out=attn_g_all[:, first : first + G_GROUP, :], in_=bank[:])
+
+        def gate(b, attn_all):
             y = y_pool.tile([P, PIX, PACK], BF16, align_bytes=64, tag="y", name="y")
             y_runs = y[:].rearrange("p (g i) j -> p g j i", i=RUN)
             x_runs = x_all[:, b, :].rearrange("p (j g i) -> p g j i", j=PACK, i=RUN)
@@ -113,7 +125,7 @@ def tile_nlgp_pb_t_kernel(tc, x, m, w_mask, out):
             nc.gpsimd.tensor_tensor(
                 out=y_runs[:, v_runs:, :, :],
                 in0=x_runs[:, v_runs:, :, :],
-                in1=attn_g[:]
+                in1=attn_g_all[:, b, :]
                 .rearrange("p (g i) -> p g i", i=RUN)
                 .unsqueeze(2)
                 .to_broadcast([P, g_runs, PACK, RUN]),
@@ -122,7 +134,7 @@ def tile_nlgp_pb_t_kernel(tc, x, m, w_mask, out):
             nc.vector.tensor_tensor(
                 out=y_runs[:, :v_runs, :, :],
                 in0=x_runs[:, :v_runs, :, :],
-                in1=attn_all[:, 0:V_PIX]
+                in1=attn_all[:]
                 .rearrange("p (g i) -> p g i", i=RUN)
                 .unsqueeze(2)
                 .to_broadcast([P, v_runs, PACK, RUN]),
@@ -150,19 +162,25 @@ def tile_nlgp_pb_t_kernel(tc, x, m, w_mask, out):
                     start=True,
                     stop=True,
                 )
-                nc.scalar.copy(out=res[:, i, :], in_=acc[:])
+                if b == B - 1 and i % 2 == 1:
+                    nc.vector.tensor_copy(out=res[:, i, :], in_=acc[:])
+                else:
+                    nc.scalar.copy(out=res[:, i, :], in_=acc[:])
             nc.sync.dma_start(
                 out=out[b].rearrange("(r i) h w -> r (i h w)", i=D_TILES),
                 in_=res[:].rearrange("r i w -> r (i w)"),
             )
 
-        attn_of = {}
-        for b in range(AHEAD):
+        attn_of = {0: spread(0)}
+        spread_for_gpsimd(0)
+        for b in range(1, AHEAD):
             attn_of[b] = spread(b)
-        y_of = {0: gate(0, *attn_of[0])}
+        y_of = {0: gate(0, attn_of[0])}
         for b in range(B):
             if b + AHEAD < B:
                 attn_of[b + AHEAD] = spread(b + AHEAD)
             if b + 1 < B:
-                y_of[b + 1] = gate(b + 1, *attn_of[b + 1])
+                y_of[b + 1] = gate(b + 1, attn_of[b + 1])
             convolve(b, y_of[b])
+            if (b + 1) * G_GROUP < B:
+                spread_for_gpsimd((b + 1) * G_GROUP)

@@ -15,7 +15,7 @@ B = 16
 C = 512
 PIX = 512
 D_TILES = C // P
-RUN = 4
+RUN = 8
 G_PIX = 96
 V_PIX = PIX - G_PIX
 LOAD_IMAGES = (1, 1, 2, 4, 4, 4)

@@ -38,7 +38,7 @@ def tile_nlgp_pb_t_kernel(tc, x, m, w_mask, out):
         psum_acc = ctx.enter_context(tc.psum_pool(name="psum_acc", bufs=ACC_BANKS))
 
         m_sb = const.tile([B, PIX], BF16)
-        nc.sync.dma_start(out=m_sb[:], in_=m)
+        nc.scalar.dma_start(out=m_sb[:], in_=m)
         w_sb = const.tile([P, D_TILES * C], BF16, align_bytes=256)
         nc.sync.dma_start(out=w_sb[:], in_=w_mask.rearrange("(r i) c -> r (i c)", i=D_TILES))
         x_all = x_pool.tile([P, B, PACK * PIX], BF16, align_bytes=256)

@@ -16,7 +16,7 @@ C = 512
 PIX = 512
 D_TILES = C // P
 RUN = 8
-G_PIX = 96
+G_PIX = 104
 V_PIX = PIX - G_PIX
 LOAD_IMAGES = (1, 1, 2, 4, 4, 4)
 G_GROUP = 4

@@ -16,7 +16,7 @@ C = 512
 PIX = 512
 D_TILES = C // P
 RUN = 8
-G_PIX = 104
+G_PIX = 112
 V_PIX = PIX - G_PIX
 LOAD_IMAGES = (1, 1, 2, 4, 4, 4)
 G_GROUP = 4

from contextlib import ExitStack

import concourse.mybir as mybir
from concourse.masks import make_identity

F32 = mybir.dt.float32
BF16 = mybir.dt.bfloat16
U32 = mybir.dt.uint32
U8 = mybir.dt.uint8
FP8X4 = mybir.dt.float8_e4m3fn_x4

P = 128
PACK = 4
B = 16
C = 512
PIX = 512
D_TILES = C // P
RUN = 8
G_PIX = 112
V_PIX = PIX - G_PIX
LOAD_IMAGES = (1, 1, 2, 4, 4, 4)
G_GROUP = 4
AHEAD = 3
ACC_BANKS = 8 - AHEAD

FLOPS = 2 * B * C * C * PIX


def tile_nlgp_pb_t_kernel(tc, x, m, w_mask, out):
    nc = tc.nc
    with ExitStack() as ctx:
        ctx.enter_context(tc.manual_schedule())
        const = ctx.enter_context(tc.tile_pool(name="const", bufs=1))
        x_pool = ctx.enter_context(tc.tile_pool(name="x_pool", bufs=1))
        y_pool = ctx.enter_context(tc.tile_pool(name="y_pool", bufs=3))
        res_pool = ctx.enter_context(tc.tile_pool(name="res_pool", bufs=12))
        psum_gate = ctx.enter_context(tc.psum_pool(name="psum_gate", bufs=AHEAD))
        psum_acc = ctx.enter_context(tc.psum_pool(name="psum_acc", bufs=ACC_BANKS))

        m_sb = const.tile([B, PIX], BF16)
        nc.scalar.dma_start(out=m_sb[:], in_=m)
        w_sb = const.tile([P, D_TILES * C], BF16, align_bytes=256)
        nc.sync.dma_start(out=w_sb[:], in_=w_mask.rearrange("(r i) c -> r (i c)", i=D_TILES))
        x_all = x_pool.tile([P, B, PACK * PIX], BF16, align_bytes=256)
        first = 0
        for count in LOAD_IMAGES:
            nc.sync.dma_start(
                out=x_all[:, first : first + count, :],
                in_=x[first : first + count].rearrange("b (p j) h w -> p b (j h w)", j=PACK),
            )
            first += count

        ident = const.tile([P, P], F32)
        make_identity(nc, ident[:])
        zero_col = const.tile([P, 1], F32)
        nc.vector.memset(zero_col[:], 0.0)
        one_col = const.tile([P, 1], F32)
        nc.scalar.activation(out=one_col[:], in_=zero_col[:], func=mybir.ActivationFunctionType.Exp)
        attn = const.tile([P, PIX], F32)
        nc.vector.memset(attn[:], 0.0)

        neg_max = const.tile([B, 1], F32)
        nc.vector.reduce_max(out=neg_max[:], in_=m_sb[:], axis=mybir.AxisListType.X, negate=True)
        e = const.tile([B, PIX], F32)
        e_sum = const.tile([B, 1], F32)
        nc.scalar.activation(
            out=e[:],
            in_=m_sb[:],
            func=mybir.ActivationFunctionType.Exp,
            bias=neg_max[:],
            scale=1.0,
            accum_out=e_sum[:],
        )
        inv_sum = const.tile([B, 1], F32)
        nc.vector.reciprocal(out=inv_sum[:], in_=e_sum[:])
        nc.vector.tensor_scalar_mul(out=attn[0:B, :], in0=e[:], scalar1=inv_sum[:])

        w_words = w_sb[:].bitcast(F32).rearrange("r (i p u) -> r i u p", i=D_TILES, u=2)
        w_grouped = const.tile([P, D_TILES * P * PACK], BF16, align_bytes=64)
        w_grouped_words = w_grouped[:].bitcast(F32).rearrange("p (i r u) -> p i r u", i=D_TILES, u=2)
        for half in range(2):
            w_t = psum_gate.tile([P, 2, 2, P], F32, tag="gate", name="w_t")
            for i2 in range(2):
                for u in range(2):
                    nc.tensor.transpose(w_t[:, i2, u, :], w_words[:, 2 * half + i2, u, :], ident[:])
            nc.scalar.copy(
                out=w_grouped_words[:, 2 * half : 2 * half + 2, :, :],
                in_=w_t[:].rearrange("p i u r -> p i r u"),
            )
        w_codes = const.tile([P, D_TILES * P], U32, align_bytes=64)
        w_scales = const.tile([P, D_TILES * P], U8, align_bytes=64)
        nc.vector.quantize_mx(out=w_codes[:].bitcast(FP8X4), scales=w_scales[:], in_=w_grouped[:])

        def spread(b):
            attn_all = psum_gate.tile([P, V_PIX], F32, tag="gate", name="attn_all")
            nc.tensor.matmul(
                out=attn_all[:],
                lhsT=ident[:, b : b + 1].to_broadcast([P, P]),
                rhs=attn[:, 0:V_PIX],
                start=True,
                stop=True,
            )
            return attn_all

        attn_g_all = const.tile([P, B, G_PIX], F32)

        def spread_for_gpsimd(first):
            bank = psum_acc.tile([P, G_GROUP, G_PIX], F32, tag="acc", name="bank")
            for n in range(G_GROUP):
                nc.tensor.matmul(
                    out=bank[:, n, :],
                    lhsT=ident[:, first + n : first + n + 1].to_broadcast([P, P]),
                    rhs=attn[:, V_PIX:PIX],
                    start=True,
                    stop=True,
                )
            nc.scalar.copy(out=attn_g_all[:, first : first + G_GROUP, :], in_=bank[:])

        def gate(b, attn_all):
            y = y_pool.tile([P, PIX, PACK], BF16, align_bytes=64, tag="y", name="y")
            y_runs = y[:].rearrange("p (g i) j -> p g j i", i=RUN)
            x_runs = x_all[:, b, :].rearrange("p (j g i) -> p g j i", j=PACK, i=RUN)
            v_runs = V_PIX // RUN
            g_runs = G_PIX // RUN
            nc.gpsimd.tensor_tensor(
                out=y_runs[:, v_runs:, :, :],
                in0=x_runs[:, v_runs:, :, :],
                in1=attn_g_all[:, b, :]
                .rearrange("p (g i) -> p g i", i=RUN)
                .unsqueeze(2)
                .to_broadcast([P, g_runs, PACK, RUN]),
                op=mybir.AluOpType.mult,
            )
            nc.vector.tensor_tensor(
                out=y_runs[:, :v_runs, :, :],
                in0=x_runs[:, :v_runs, :, :],
                in1=attn_all[:]
                .rearrange("p (g i) -> p g i", i=RUN)
                .unsqueeze(2)
                .to_broadcast([P, v_runs, PACK, RUN]),
                op=mybir.AluOpType.mult,
            )
            return y

        def convolve(b, y):
            y_codes = y_pool.tile([P, PIX], U32, align_bytes=64, tag="y_codes", name="y_codes")
            y_scales = y_pool.tile([P, PIX], U8, align_bytes=64, tag="y_scales", name="y_scales")
            nc.vector.quantize_mx(
                out=y_codes[:].bitcast(FP8X4),
                scales=y_scales[:],
                in_=y[:].rearrange("p w j -> p (w j)"),
            )
            res = res_pool.tile([P, D_TILES, PIX], F32, align_bytes=256, tag="res", name="res")
            for i in range(D_TILES):
                acc = psum_acc.tile([P, PIX], F32, tag="acc", name="acc")
                nc.tensor.matmul_mx(
                    out=acc[:],
                    lhsT=w_codes[:, i * P : (i + 1) * P].bitcast(FP8X4),
                    lhsT_scale=w_scales[:, i * P : (i + 1) * P],
                    rhs=y_codes[:].bitcast(FP8X4),
                    rhs_scale=y_scales[:],
                    start=True,
                    stop=True,
                )
                if b == B - 1 and i % 2 == 1:
                    nc.vector.tensor_copy(out=res[:, i, :], in_=acc[:])
                else:
                    nc.scalar.copy(out=res[:, i, :], in_=acc[:])
            nc.sync.dma_start(
                out=out[b].rearrange("(r i) h w -> r (i h w)", i=D_TILES),
                in_=res[:].rearrange("r i w -> r (i w)"),
            )

        attn_of = {0: spread(0)}
        spread_for_gpsimd(0)
        for b in range(1, AHEAD):
            attn_of[b] = spread(b)
        y_of = {0: gate(0, attn_of[0])}
        for b in range(B):
            if b + AHEAD < B:
                attn_of[b + AHEAD] = spread(b + AHEAD)
            if b + 1 < B:
                y_of[b + 1] = gate(b + 1, attn_of[b + 1])
            convolve(b, y_of[b])
            if (b + 1) * G_GROUP < B:
                spread_for_gpsimd((b + 1) * G_GROUP)
